import numpy as np
import ml_dtypes


def mxq(x, axis, fmt="e4m3"):
    dtype, down = {"e4m3": (ml_dtypes.float8_e4m3fn, 7), "e5m2": (ml_dtypes.float8_e5m2, 14)}[fmt]
    v = np.moveaxis(np.asarray(x, np.float32).astype(ml_dtypes.bfloat16).astype(np.float64), axis, -1)
    blocks = v.reshape(v.shape[:-1] + (-1, 32))
    amax = np.abs(blocks).max(-1, keepdims=True)
    byte = np.maximum(np.where(amax > 0, np.frexp(amax)[1] - 1 + 127, 0) - down, 1)
    scale = np.exp2(byte - 127.0)
    codes = (blocks / scale).astype(np.float32).astype(dtype).astype(np.float64)
    return np.moveaxis((codes * scale).reshape(v.shape), -1, axis)


WIDE = False


def mx_kscale(k):
    if not WIDE:
        return np.ones(k)
    levels = np.array([10, -10, 5, -5, 0])
    a = np.random.permutation(np.resize(levels, k // 512 * 4)).reshape(k // 512, 4)
    idx = np.arange(k)
    return np.exp2(a[idx // 512, idx % 128 // 32])


BF16 = ml_dtypes.bfloat16


def bf(x):
    return np.asarray(x, np.float32).astype(BF16)


def f64(x):
    return np.asarray(x).astype(np.float64)


B, C, H, W, K = 8, 512, 32, 32, 128
N = H * W
XS = 1.6 / C ** 0.25
CS = 0.4 / C ** 0.25


def setup_inputs():
    s = mx_kscale(C)
    return {'x': bf(np.random.standard_normal((B, C, H, W)) * s[None, :, None, None]),
            'conv_w': bf(np.random.standard_normal((C, C)) * XS / np.sqrt(C) / s[None, :]),
            'conv_b': bf(np.random.standard_normal(C) * 0.4 * XS),
            'codebook': bf(np.random.standard_normal((K, C)) * CS),
            'log_smooth': bf(np.random.standard_normal(K) * 0.25 / np.sqrt(C))}


def reference(x, conv_w, conv_b, codebook, log_smooth):
    x, conv_w, conv_b, codebook, log_smooth = f64(x), f64(conv_w), f64(conv_b), f64(codebook), f64(log_smooth)
    b, c, h, w = x.shape
    xp = (mxq(conv_w, 1, 'e4m3') @ mxq(x.reshape(b, c, h * w), 1, 'e4m3')) + conv_b[None, :, None]
    xp = xp.transpose(0, 2, 1)
    smooth = np.exp(log_smooth)
    x2 = np.sum(xp * xp, axis=-1)
    c2 = np.sum(codebook * codebook, axis=-1)
    xc = mxq(xp, 2, 'e4m3') @ mxq(codebook, 1, 'e4m3').T
    dist_sq = x2[:, :, None] - 2.0 * xc + c2[None, None, :]
    z = -smooth[None, None, :] * dist_sq
    ez = np.exp(z - z.max(axis=2, keepdims=True))
    assign = ez / ez.sum(axis=2, keepdims=True)
    return xp, assign

@@ -1,0 +1,332 @@
+from contextlib import ExitStack
+
+import concourse.mybir as mybir
+from concourse.masks import make_identity
+
+F32 = mybir.dt.float32
+BF16 = mybir.dt.bfloat16
+U32 = mybir.dt.uint32
+U8 = mybir.dt.uint8
+FP8X4 = mybir.dt.float8_e4m3fn_x4
+ACT = mybir.ActivationFunctionType
+ALU = mybir.AluOpType
+
+P = 128
+IMAGES = 8
+CH = 512
+PIXELS = 1024
+WORDS = 128
+GROUP = 512
+TILES = GROUP // P
+GROUPS = IMAGES * PIXELS // GROUP
+
+FLOPS = 2 * IMAGES * PIXELS * CH * CH + 2 * IMAGES * PIXELS * CH * WORDS
+
+
+def tile_lvc_pa_t_kernel(tc, x, conv_w, conv_b, codebook, log_smooth, out_0, out_1):
+    nc = tc.nc
+    with ExitStack() as ctx:
+        ctx.enter_context(tc.manual_schedule())
+        const = ctx.enter_context(tc.tile_pool(name="const", bufs=1))
+        xin = ctx.enter_context(tc.tile_pool(name="xin", bufs=1))
+        two = ctx.enter_context(tc.tile_pool(name="two", bufs=2))
+        three = ctx.enter_context(tc.tile_pool(name="three", bufs=3))
+        four = ctx.enter_context(tc.tile_pool(name="four", bufs=4))
+        psum_y = ctx.enter_context(tc.psum_pool(name="psum_y", bufs=4))
+        psum_t = ctx.enter_context(tc.psum_pool(name="psum_t", bufs=3))
+        psum_c = ctx.enter_context(tc.psum_pool(name="psum_c", bufs=1))
+
+        w_raw = const.tile([P, 4 * CH], BF16)
+        nc.sync.dma_start(
+            out=w_raw[:].rearrange("p (a c) -> p a c", a=4),
+            in_=conv_w.rearrange("(a p) c -> p a c", p=P),
+        )
+        cb_raw = const.tile([P, CH], BF16)
+        nc.scalar.dma_start(out=cb_raw[:], in_=codebook)
+
+        zrow = const.tile([P, 768], BF16)
+        nc.vector.memset(zrow[:], 0.0)
+        ones = const.tile([P, P], BF16)
+        nc.vector.memset(ones[:], 1.0)
+        warm_in = const.tile([P, 1], F32)
+        nc.vector.memset(warm_in[:], 0.0)
+        nc.scalar.dma_start(out=zrow[0:1, 0:CH], in_=conv_b.rearrange("(o c) -> o c", o=1))
+        nc.scalar.dma_start(out=zrow[0:1, CH : CH + WORDS], in_=log_smooth.rearrange("(o c) -> o c", o=1))
+
+        raw = [xin.tile([P, 4, PIXELS], BF16, name="raw%d" % b) for b in range(IMAGES)]
+        x0 = x[0].rearrange("(u p e) h w -> u p e (h w)", u=2, p=P, e=2)
+        for half in range(2):
+            for u in range(2):
+                nc.sync.dma_start(
+                    out=raw[0][:, 2 * u : 2 * u + 2, GROUP * half : GROUP * (half + 1)],
+                    in_=x0[u][:, :, GROUP * half : GROUP * (half + 1)],
+                )
+        for b in range(1, IMAGES):
+            nc.sync.dma_start(
+                out=raw[b][:].rearrange("p (u e) n -> p u (e n)", u=2),
+                in_=x[b].rearrange("(u p e) h w -> p u (e h w)", u=2, p=P, e=2),
+            )
+
+        ident = const.tile([P, P], F32)
+        make_identity(nc, ident[:])
+
+        warm_out = const.tile([P, 1], F32)
+        nc.scalar.activation(out=warm_out[:], in_=warm_in[:], func=ACT.Exp)
+
+        cb_f32 = const.tile([P, CH], F32)
+        nc.scalar.copy(out=cb_f32[:], in_=cb_raw[:])
+        cb_t = psum_t.tile([P, 4, P], F32, tag="xt")
+        for t in range(4):
+            nc.tensor.transpose(cb_t[:, t, :], cb_f32[:, P * t : P * (t + 1)], ident[:])
+        cb_sq = const.tile([P, CH], BF16)
+        c2col = const.tile([P, 1], F32)
+        nc.scalar.activation(out=cb_sq[:], in_=cb_raw[:], func=ACT.Square, accum_out=c2col[:])
+        c2rep = const.tile([P, P], F32)
+        nc.scalar.copy(out=c2rep[:], in_=c2col[:, 0:1].to_broadcast([P, P]))
+        cb_grouped = const.tile([P, WORDS, 4], BF16, align_bytes=64)
+        nc.scalar.copy(out=cb_grouped[:], in_=cb_t[:].rearrange("p t k -> p k t"))
+
+        w_words = w_raw[:].bitcast(F32)
+        w_grouped = const.tile([P, 4 * CH], BF16, align_bytes=64)
+        w_grouped_words = w_grouped[:].bitcast(F32)
+        for h in range(2):
+            w_t = psum_t.tile([P, 4, P], F32, tag="xt")
+            for a in range(2):
+                for u in range(2):
+                    col = (2 * h + a) * 256 + u * P
+                    nc.tensor.transpose(w_t[:, 2 * a + u, :], w_words[:, col : col + P], ident[:])
+            dst = w_grouped_words[:, 512 * h : 512 * (h + 1)].rearrange("p (a o u) -> p a o u", a=2, u=2)
+            src = w_t[:].rearrange("p (a u) o -> p a o u", a=2)
+            if h == 0:
+                nc.vector.tensor_copy(out=dst, in_=src)
+            else:
+                nc.scalar.copy(out=dst, in_=src)
+
+        cb_codes = const.tile([P, WORDS], U32, align_bytes=64)
+        cb_scales = const.tile([P, WORDS], U8, align_bytes=64)
+        nc.vector.quantize_mx(
+            out=cb_codes[:].bitcast(FP8X4), scales=cb_scales[:], in_=cb_grouped[:].rearrange("p k t -> p (k t)")
+        )
+
+        x_grouped = {}
+        x_codes = {}
+        x_scales = {}
+        y_banks = {}
+        xp = {}
+        x2 = {}
+        xt_banks = {}
+        xp_grouped = {}
+        xp_codes = {}
+        xp_scales = {}
+        xc_banks = {}
+        dist = {}
+        dmin = {}
+        expo = {}
+        esum = {}
+        rsum = {}
+
+        def live(g):
+            return 0 <= g < GROUPS
+
+        def regroup_x(g):
+            if not live(g):
+                return
+            n0 = GROUP * (g % 2)
+            grouped = two.tile([P, GROUP, 4], BF16, align_bytes=64, tag="x_grouped")
+            nc.vector.tensor_copy(
+                out=grouped[:].rearrange("p (c i) t -> p c t i", i=4),
+                in_=raw[g // 2][:, :, n0 : n0 + GROUP].rearrange("p t (c i) -> p c t i", i=4),
+            )
+            x_grouped[g] = grouped
+
+        def quantise_x(g):
+            if not live(g):
+                return
+            codes = two.tile([P, GROUP], U32, align_bytes=64, tag="x_codes")
+            scales = two.tile([P, GROUP], U8, align_bytes=64, tag="x_scales")
+            nc.vector.quantize_mx(
+                out=codes[:].bitcast(FP8X4), scales=scales[:], in_=x_grouped[g][:].rearrange("p n t -> p (n t)")
+            )
+            x_codes[g] = codes
+            x_scales[g] = scales
+
+        def conv(g):
+            if not live(g):
+                return
+            for j in range(TILES):
+                y = psum_y.tile([P, CH], F32, tag="y")
+                nc.tensor.matmul_mx(
+                    out=y[:],
+                    lhsT=x_codes[g][:, P * j : P * (j + 1)].bitcast(FP8X4),
+                    lhsT_scale=x_scales[g][:, P * j : P * (j + 1)],
+                    rhs=w_codes[:].bitcast(FP8X4),
+                    rhs_scale=w_scales[:],
+                    start=True,
+                    stop=True,
+                )
+                y_banks[(g, j)] = y
+
+        def add_bias(g, j):
+            if j == 0:
+                xp_tile = three.tile([P, TILES, CH], F32, tag="xp")
+                xp[g] = xp_tile
+                x2_tile = four.tile([P, TILES], F32, tag="x2")
+                x2[g] = x2_tile
+                grouped = two.tile([P, TILES, P, 4], BF16, align_bytes=64, tag="xp_grouped")
+                xp_grouped[g] = grouped
+            nc.vector.tensor_tensor(out=xp[g][:, j, :], in0=y_banks[(g, j)][:], in1=bias_bc[:], op=ALU.add)
+
+        def transposes(g, j):
+            xt = psum_t.tile([P, 4, P], F32, tag="xt")
+            for t in range(4):
+                nc.tensor.transpose(xt[:, t, :], xp[g][:, j, P * t : P * (t + 1)], ident[:])
+            xt_banks[(g, j)] = xt
+
+        def sum_squares(g, j):
+            junk = two.tile([P, CH], BF16, tag="junk")
+            nc.scalar.activation(out=junk[:], in_=xp[g][:, j, :], func=ACT.Square, accum_out=x2[g][:, j : j + 1])
+
+        def regroup_xp(g, j):
+            nc.scalar.copy(out=xp_grouped[g][:, j, :, :], in_=xt_banks[(g, j)][:].rearrange("p t n -> p n t"))
+
+        def store_xp(g):
+            n0 = GROUP * (g % 2)
+            nc.sync.dma_start(
+                out=out_0[g // 2, n0 : n0 + GROUP, :].rearrange("(j p) o -> p j o", p=P), in_=xp[g][:]
+            )
+
+        def quantise_xp(g):
+            if not live(g):
+                return
+            codes = two.tile([P, GROUP], U32, align_bytes=64, tag="xp_codes")
+            scales = two.tile([P, GROUP], U8, align_bytes=64, tag="xp_scales")
+            nc.vector.quantize_mx(
+                out=codes[:].bitcast(FP8X4),
+                scales=scales[:],
+                in_=xp_grouped[g][:].rearrange("p j n t -> p (j n t)"),
+            )
+            xp_codes[g] = codes
+            xp_scales[g] = scales
+
+        def cross(g):
+            if not live(g):
+                return
+            xc = psum_c.tile([P, TILES, WORDS], F32, tag="xc")
+            for j in range(TILES):
+                nc.tensor.matmul_mx(
+                    out=xc[:, j, :],
+                    lhsT=xp_codes[g][:, P * j : P * (j + 1)].bitcast(FP8X4),
+                    lhsT_scale=xp_scales[g][:, P * j : P * (j + 1)],
+                    rhs=cb_codes[:].bitcast(FP8X4),
+                    rhs_scale=cb_scales[:],
+                    start=True,
+                    stop=True,
+                )
+            xc_banks[g] = xc
+
+        def distances(g):
+            if not live(g):
+                return
+            part = two.tile([P, TILES, WORDS], F32, tag="part")
+            nc.vector.scalar_tensor_tensor(
+                out=part[:].rearrange("p j k -> p (j k)"),
+                in0=xc_banks[g][:].rearrange("p j k -> p (j k)"),
+                scalar=-2.0,
+                in1=c2_bc[:].rearrange("p j k -> p (j k)"),
+                op0=ALU.mult,
+                op1=ALU.add,
+            )
+            scaled = two.tile([P, TILES, WORDS], F32, tag="scaled")
+            for j in range(TILES):
+                nc.vector.scalar_tensor_tensor(
+                    out=scaled[:, j, :],
+                    in0=part[:, j, :],
+                    scalar=x2[g][:, j : j + 1],
+                    in1=s_bc[:],
+                    op0=ALU.add,
+                    op1=ALU.mult,
+                )
+            least = three.tile([P, TILES], F32, tag="least")
+            nc.vector.tensor_reduce(out=least[:], in_=scaled[:], axis=mybir.AxisListType.X, op=ALU.min)
+            dist[g] = scaled
+            dmin[g] = least
+
+        def exponent(g):
+            if not live(g):
+                return
+            e = two.tile([P, TILES, WORDS], F32, tag="expo")
+            total = three.tile([P, TILES], F32, tag="esum")
+            for j in range(TILES):
+                nc.scalar.activation(
+                    out=e[:, j, :],
+                    in_=dist[g][:, j, :],
+                    func=ACT.Exp,
+                    bias=dmin[g][:, j : j + 1],
+                    scale=-1.0,
+                    accum_out=total[:, j : j + 1],
+                )
+            expo[g] = e
+            esum[g] = total
+
+        def reciprocal(g):
+            if not live(g):
+                return
+            r = three.tile([P, TILES], F32, tag="rsum")
+            nc.vector.reciprocal(out=r[:], in_=esum[g][:])
+            rsum[g] = r
+
+        def normalise(g):
+            if not live(g):
+                return
+            assign = three.tile([P, TILES, WORDS], F32, tag="assign")
+            for j in range(TILES):
+                nc.scalar.activation(
+                    out=assign[:, j, :], in_=expo[g][:, j, :], func=ACT.Copy, scale=rsum[g][:, j : j + 1]
+                )
+            n0 = GROUP * (g % 2)
+            nc.sync.dma_start(
+                out=out_1[g // 2, n0 : n0 + GROUP, :].rearrange("(j p) k -> p j k", p=P), in_=assign[:]
+            )
+
+        regroup_x(0)
+        w_codes = const.tile([P, CH], U32, align_bytes=64)
+        w_scales = const.tile([P, CH], U8, align_bytes=64)
+        nc.vector.quantize_mx(out=w_codes[:].bitcast(FP8X4), scales=w_scales[:], in_=w_grouped[:])
+        regroup_x(1)
+        quantise_x(0)
+
+        bias_ps = psum_y.tile([P, CH], F32, tag="y")
+        nc.tensor.matmul(out=bias_ps[:], lhsT=ones[:], rhs=zrow[:, 0:CH], start=True, stop=True)
+        bias_bc = const.tile([P, CH], F32)
+        nc.scalar.copy(out=bias_bc[:], in_=bias_ps[:])
+        ls_ps = psum_t.tile([P, 4, P], F32, tag="xt")
+        nc.tensor.matmul(
+            out=ls_ps[:, 0:2, :].rearrange("p a k -> p (a k)"), lhsT=ones[:], rhs=zrow[:, CH:768], start=True, stop=True
+        )
+        s_bc = const.tile([P, WORDS], F32)
+        nc.scalar.activation(out=s_bc[:], in_=ls_ps[:, 0, :], func=ACT.Exp)
+        c2_ps = psum_c.tile([P, TILES, WORDS], F32, tag="xc")
+        nc.tensor.transpose(c2_ps[:, 0, :], c2rep[:], ident[:])
+        c2_bc = const.tile([P, TILES, WORDS], F32)
+        nc.scalar.copy(out=c2_bc[:], in_=c2_ps[:, 0:1, :].to_broadcast([P, TILES, WORDS]))
+        conv(0)
+
+        for it in range(GROUPS + 5):
+            normalise(it - 4)
+            exponent(it - 3)
+            if live(it):
+                for j in range(TILES):
+                    add_bias(it, j)
+                    transposes(it, j)
+                    sum_squares(it, j)
+                    if j >= 1:
+                        regroup_xp(it, j - 1)
+                regroup_xp(it, TILES - 1)
+                store_xp(it)
+            quantise_x(it + 1)
+            conv(it + 1)
+            distances(it - 2)
+            quantise_xp(it - 1)
+            cross(it - 1)
+            regroup_x(it + 2)
+            reciprocal(it - 3)

@@ -26,7 +26,6 @@ FLOPS = 2 * IMAGES * PIXELS * CH * CH + 2 * IMAGES * PIXELS * CH * WORDS
 def tile_lvc_pa_t_kernel(tc, x, conv_w, conv_b, codebook, log_smooth, out_0, out_1):
     nc = tc.nc
     with ExitStack() as ctx:
-        ctx.enter_context(tc.manual_schedule())
         const = ctx.enter_context(tc.tile_pool(name="const", bufs=1))
         xin = ctx.enter_context(tc.tile_pool(name="xin", bufs=1))
         two = ctx.enter_context(tc.tile_pool(name="two", bufs=2))

@@ -19,6 +19,7 @@ WORDS = 128
 GROUP = 512
 TILES = GROUP // P
 GROUPS = IMAGES * PIXELS // GROUP
+VECTOR_REGROUPS = 2
 
 FLOPS = 2 * IMAGES * PIXELS * CH * CH + 2 * IMAGES * PIXELS * CH * WORDS
 
@@ -132,10 +133,20 @@ def tile_lvc_pa_t_kernel(tc, x, conv_w, conv_b, codebook, log_smooth, out_0, out
                 return
             n0 = GROUP * (g % 2)
             grouped = two.tile([P, GROUP, 4], BF16, align_bytes=64, tag="x_grouped")
-            nc.vector.tensor_copy(
-                out=grouped[:].rearrange("p (c i) t -> p c t i", i=4),
-                in_=raw[g // 2][:, :, n0 : n0 + GROUP].rearrange("p t (c i) -> p c t i", i=4),
-            )
+            if g < VECTOR_REGROUPS:
+                nc.vector.tensor_copy(
+                    out=grouped[:].rearrange("p (c i) t -> p c t i", i=4),
+                    in_=raw[g // 2][:, :, n0 : n0 + GROUP].rearrange("p t (c i) -> p c t i", i=4),
+                )
+            else:
+                nc.gpsimd.tensor_scalar(
+                    out=grouped[:],
+                    in0=raw[g // 2][:, :, n0 : n0 + GROUP].rearrange("p t n -> p n t"),
+                    scalar1=1.0,
+                    scalar2=0.0,
+                    op0=ALU.mult,
+                    op1=ALU.add,
+                )
             x_grouped[g] = grouped
 
         def quantise_x(g):
@@ -186,7 +197,12 @@ def tile_lvc_pa_t_kernel(tc, x, conv_w, conv_b, codebook, log_smooth, out_0, out
             nc.scalar.activation(out=junk[:], in_=xp[g][:, j, :], func=ACT.Square, accum_out=x2[g][:, j : j + 1])
 
         def regroup_xp(g, j):
-            nc.scalar.copy(out=xp_grouped[g][:, j, :, :], in_=xt_banks[(g, j)][:].rearrange("p t n -> p n t"))
+            if j == TILES - 1 and g % 4 != 0:
+                nc.vector.tensor_copy(
+                    out=xp_grouped[g][:, j, :, :], in_=xt_banks[(g, j)][:].rearrange("p t n -> p n t")
+                )
+            else:
+                nc.scalar.copy(out=xp_grouped[g][:, j, :, :], in_=xt_banks[(g, j)][:].rearrange("p t n -> p n t"))
 
         def store_xp(g):
             n0 = GROUP * (g % 2)

@@ -19,6 +19,7 @@ WORDS = 128
 GROUP = 512
 TILES = GROUP // P
 GROUPS = IMAGES * PIXELS // GROUP
+LAG = 2
 VECTOR_REGROUPS = 2
 
 FLOPS = 2 * IMAGES * PIXELS * CH * CH + 2 * IMAGES * PIXELS * CH * WORDS
@@ -32,9 +33,10 @@ def tile_lvc_pa_t_kernel(tc, x, conv_w, conv_b, codebook, log_smooth, out_0, out
         two = ctx.enter_context(tc.tile_pool(name="two", bufs=2))
         three = ctx.enter_context(tc.tile_pool(name="three", bufs=3))
         four = ctx.enter_context(tc.tile_pool(name="four", bufs=4))
-        psum_y = ctx.enter_context(tc.psum_pool(name="psum_y", bufs=4))
+        psum_y = ctx.enter_context(tc.psum_pool(name="psum_y", bufs=3))
         psum_t = ctx.enter_context(tc.psum_pool(name="psum_t", bufs=3))
         psum_c = ctx.enter_context(tc.psum_pool(name="psum_c", bufs=1))
+        psum_s = ctx.enter_context(tc.psum_pool(name="psum_s", bufs=1))
 
         w_raw = const.tile([P, 4 * CH], BF16)
         nc.sync.dma_start(
@@ -44,9 +46,9 @@ def tile_lvc_pa_t_kernel(tc, x, conv_w, conv_b, codebook, log_smooth, out_0, out
         cb_raw = const.tile([P, CH], BF16)
         nc.scalar.dma_start(out=cb_raw[:], in_=codebook)
 
-        zrow = const.tile([P, 768], BF16)
+        zrow = const.tile([P, CH + WORDS], BF16)
         nc.vector.memset(zrow[:], 0.0)
-        ones = const.tile([P, P], BF16)
+        ones = const.tile([P, 2 * P], BF16)
         nc.vector.memset(ones[:], 1.0)
         warm_in = const.tile([P, 1], F32)
         nc.vector.memset(warm_in[:], 0.0)
@@ -108,16 +110,13 @@ def tile_lvc_pa_t_kernel(tc, x, conv_w, conv_b, codebook, log_smooth, out_0, out
             out=cb_codes[:].bitcast(FP8X4), scales=cb_scales[:], in_=cb_grouped[:].rearrange("p k t -> p (k t)")
         )
 
-        x_grouped = {}
-        x_codes = {}
-        x_scales = {}
+        grouped = {}
+        codes = {}
+        scales = {}
         y_banks = {}
         xp = {}
         x2 = {}
         xt_banks = {}
-        xp_grouped = {}
-        xp_codes = {}
-        xp_scales = {}
         xc_banks = {}
         dist = {}
         dmin = {}
@@ -128,37 +127,46 @@ def tile_lvc_pa_t_kernel(tc, x, conv_w, conv_b, codebook, log_smooth, out_0, out
         def live(g):
             return 0 <= g < GROUPS
 
+        def grouped_tile(m):
+            if m not in grouped:
+                pair = three.tile([P, 2, GROUP * 4], BF16, align_bytes=64, tag="grouped")
+                grouped[m] = pair
+            return grouped[m]
+
         def regroup_x(g):
             if not live(g):
                 return
             n0 = GROUP * (g % 2)
-            grouped = two.tile([P, GROUP, 4], BF16, align_bytes=64, tag="x_grouped")
+            half = grouped_tile(g)[:, 0, :].rearrange("p (n t) -> p n t", t=4)
             if g < VECTOR_REGROUPS:
                 nc.vector.tensor_copy(
-                    out=grouped[:].rearrange("p (c i) t -> p c t i", i=4),
+                    out=half.rearrange("p (c i) t -> p c t i", i=4),
                     in_=raw[g // 2][:, :, n0 : n0 + GROUP].rearrange("p t (c i) -> p c t i", i=4),
                 )
             else:
                 nc.gpsimd.tensor_scalar(
-                    out=grouped[:],
+                    out=half,
                     in0=raw[g // 2][:, :, n0 : n0 + GROUP].rearrange("p t n -> p n t"),
                     scalar1=1.0,
                     scalar2=0.0,
                     op0=ALU.mult,
                     op1=ALU.add,
                 )
-            x_grouped[g] = grouped
 
-        def quantise_x(g):
-            if not live(g):
+        def quantise(m):
+            lo = 0 if live(m) else 1
+            hi = 2 if live(m - LAG) else 1
+            if lo >= hi:
                 return
-            codes = two.tile([P, GROUP], U32, align_bytes=64, tag="x_codes")
-            scales = two.tile([P, GROUP], U8, align_bytes=64, tag="x_scales")
+            c_tile = two.tile([P, 2, GROUP], U32, align_bytes=64, tag="codes")
+            s_tile = two.tile([P, 2, GROUP], U8, align_bytes=64, tag="scales")
             nc.vector.quantize_mx(
-                out=codes[:].bitcast(FP8X4), scales=scales[:], in_=x_grouped[g][:].rearrange("p n t -> p (n t)")
+                out=c_tile[:, lo:hi, :].rearrange("p a n -> p (a n)").bitcast(FP8X4),
+                scales=s_tile[:, lo:hi, :].rearrange("p a n -> p (a n)"),
+                in_=grouped[m][:, lo:hi, :].rearrange("p a n -> p (a n)"),
             )
-            x_codes[g] = codes
-            x_scales[g] = scales
+            codes[m] = c_tile
+            scales[m] = s_tile
 
         def conv(g):
             if not live(g):
@@ -167,8 +175,8 @@ def tile_lvc_pa_t_kernel(tc, x, conv_w, conv_b, codebook, log_smooth, out_0, out
                 y = psum_y.tile([P, CH], F32, tag="y")
                 nc.tensor.matmul_mx(
                     out=y[:],
-                    lhsT=x_codes[g][:, P * j : P * (j + 1)].bitcast(FP8X4),
-                    lhsT_scale=x_scales[g][:, P * j : P * (j + 1)],
+                    lhsT=codes[g][:, 0, P * j : P * (j + 1)].bitcast(FP8X4),
+                    lhsT_scale=scales[g][:, 0, P * j : P * (j + 1)],
                     rhs=w_codes[:].bitcast(FP8X4),
                     rhs_scale=w_scales[:],
                     start=True,
@@ -182,8 +190,6 @@ def tile_lvc_pa_t_kernel(tc, x, conv_w, conv_b, codebook, log_smooth, out_0, out
                 xp[g] = xp_tile
                 x2_tile = four.tile([P, TILES], F32, tag="x2")
                 x2[g] = x2_tile
-                grouped = two.tile([P, TILES, P, 4], BF16, align_bytes=64, tag="xp_grouped")
-                xp_grouped[g] = grouped
             nc.vector.tensor_tensor(out=xp[g][:, j, :], in0=y_banks[(g, j)][:], in1=bias_bc[:], op=ALU.add)
 
         def transposes(g, j):
@@ -197,31 +203,18 @@ def tile_lvc_pa_t_kernel(tc, x, conv_w, conv_b, codebook, log_smooth, out_0, out
             nc.scalar.activation(out=junk[:], in_=xp[g][:, j, :], func=ACT.Square, accum_out=x2[g][:, j : j + 1])
 
         def regroup_xp(g, j):
+            dst = grouped_tile(g + LAG)[:, 1, 4 * P * j : 4 * P * (j + 1)].rearrange("p (n t) -> p n t", t=4)
+            src = xt_banks[(g, j)][:].rearrange("p t n -> p n t")
             if j == TILES - 1 and g % 4 != 0:
-                nc.vector.tensor_copy(
-                    out=xp_grouped[g][:, j, :, :], in_=xt_banks[(g, j)][:].rearrange("p t n -> p n t")
-                )
+                nc.vector.tensor_copy(out=dst, in_=src)
             else:
-                nc.scalar.copy(out=xp_grouped[g][:, j, :, :], in_=xt_banks[(g, j)][:].rearrange("p t n -> p n t"))
+                nc.scalar.copy(out=dst, in_=src)
 
         def store_xp(g):
             n0 = GROUP * (g % 2)
             nc.sync.dma_start(
                 out=out_0[g // 2, n0 : n0 + GROUP, :].rearrange("(j p) o -> p j o", p=P), in_=xp[g][:]
             )
-
-        def quantise_xp(g):
-            if not live(g):
-                return
-            codes = two.tile([P, GROUP], U32, align_bytes=64, tag="xp_codes")
-            scales = two.tile([P, GROUP], U8, align_bytes=64, tag="xp_scales")
-            nc.vector.quantize_mx(
-                out=codes[:].bitcast(FP8X4),
-                scales=scales[:],
-                in_=xp_grouped[g][:].rearrange("p j n t -> p (j n t)"),
-            )
-            xp_codes[g] = codes
-            xp_scales[g] = scales
 
         def cross(g):
             if not live(g):
@@ -230,8 +223,8 @@ def tile_lvc_pa_t_kernel(tc, x, conv_w, conv_b, codebook, log_smooth, out_0, out
             for j in range(TILES):
                 nc.tensor.matmul_mx(
                     out=xc[:, j, :],
-                    lhsT=xp_codes[g][:, P * j : P * (j + 1)].bitcast(FP8X4),
-                    lhsT_scale=xp_scales[g][:, P * j : P * (j + 1)],
+                    lhsT=codes[g + LAG][:, 1, P * j : P * (j + 1)].bitcast(FP8X4),
+                    lhsT_scale=scales[g + LAG][:, 1, P * j : P * (j + 1)],
                     rhs=cb_codes[:].bitcast(FP8X4),
                     rhs_scale=cb_scales[:],
                     start=True,
@@ -257,7 +250,7 @@ def tile_lvc_pa_t_kernel(tc, x, conv_w, conv_b, codebook, log_smooth, out_0, out
                     out=scaled[:, j, :],
                     in0=part[:, j, :],
                     scalar=x2[g][:, j : j + 1],
-                    in1=s_bc[:],
+                    in1=s_ps[:, 0:WORDS],
                     op0=ALU.add,
                     op1=ALU.mult,
                 )
@@ -295,9 +288,19 @@ def tile_lvc_pa_t_kernel(tc, x, conv_w, conv_b, codebook, log_smooth, out_0, out
                 return
             assign = three.tile([P, TILES, WORDS], F32, tag="assign")
             for j in range(TILES):
-                nc.scalar.activation(
-                    out=assign[:, j, :], in_=expo[g][:, j, :], func=ACT.Copy, scale=rsum[g][:, j : j + 1]
-                )
+                if False:
+                    nc.gpsimd.tensor_scalar(
+                        out=assign[:, j, :],
+                        in0=expo[g][:, j, :],
+                        scalar1=rsum[g][:, j : j + 1],
+                        scalar2=0.0,
+                        op0=ALU.mult,
+                        op1=ALU.add,
+                    )
+                else:
+                    nc.scalar.activation(
+                        out=assign[:, j, :], in_=expo[g][:, j, :], func=ACT.Copy, scale=rsum[g][:, j : j + 1]
+                    )
             n0 = GROUP * (g % 2)
             nc.sync.dma_start(
                 out=out_1[g // 2, n0 : n0 + GROUP, :].rearrange("(j p) k -> p j k", p=P), in_=assign[:]
@@ -308,18 +311,24 @@ def tile_lvc_pa_t_kernel(tc, x, conv_w, conv_b, codebook, log_smooth, out_0, out
         w_scales = const.tile([P, CH], U8, align_bytes=64)
         nc.vector.quantize_mx(out=w_codes[:].bitcast(FP8X4), scales=w_scales[:], in_=w_grouped[:])
         regroup_x(1)
-        quantise_x(0)
+        quantise(0)
 
         bias_ps = psum_y.tile([P, CH], F32, tag="y")
-        nc.tensor.matmul(out=bias_ps[:], lhsT=ones[:], rhs=zrow[:, 0:CH], start=True, stop=True)
+        nc.tensor.matmul(out=bias_ps[:], lhsT=ones[:, 0:P], rhs=zrow[:, 0:CH], start=True, stop=True)
         bias_bc = const.tile([P, CH], F32)
         nc.scalar.copy(out=bias_bc[:], in_=bias_ps[:])
         ls_ps = psum_t.tile([P, 4, P], F32, tag="xt")
         nc.tensor.matmul(
-            out=ls_ps[:, 0:2, :].rearrange("p a k -> p (a k)"), lhsT=ones[:], rhs=zrow[:, CH:768], start=True, stop=True
+            out=ls_ps[:, 0:2, :].rearrange("p a k -> p (a k)"),
+            lhsT=zrow[:, CH : CH + WORDS],
+            rhs=ones[:],
+            start=True,
+            stop=True,
         )
-        s_bc = const.tile([P, WORDS], F32)
-        nc.scalar.activation(out=s_bc[:], in_=ls_ps[:, 0, :], func=ACT.Exp)
+        s_rep = const.tile([P, P], F32)
+        nc.scalar.activation(out=s_rep[:], in_=ls_ps[:, 0, :], func=ACT.Exp)
+        s_ps = psum_s.tile([P, CH], F32, tag="s")
+        nc.tensor.transpose(s_ps[:, 0:WORDS], s_rep[:], ident[:])
         c2_ps = psum_c.tile([P, TILES, WORDS], F32, tag="xc")
         nc.tensor.transpose(c2_ps[:, 0, :], c2rep[:], ident[:])
         c2_bc = const.tile([P, TILES, WORDS], F32)
@@ -338,10 +347,9 @@ def tile_lvc_pa_t_kernel(tc, x, conv_w, conv_b, codebook, log_smooth, out_0, out
                         regroup_xp(it, j - 1)
                 regroup_xp(it, TILES - 1)
                 store_xp(it)
-            quantise_x(it + 1)
+            quantise(it + 1)
             conv(it + 1)
             distances(it - 2)
-            quantise_xp(it - 1)
             cross(it - 1)
             regroup_x(it + 2)
             reciprocal(it - 3)

@@ -19,7 +19,6 @@ WORDS = 128
 GROUP = 512
 TILES = GROUP // P
 GROUPS = IMAGES * PIXELS // GROUP
-LAG = 2
 VECTOR_REGROUPS = 2
 
 FLOPS = 2 * IMAGES * PIXELS * CH * CH + 2 * IMAGES * PIXELS * CH * WORDS
@@ -28,15 +27,16 @@ FLOPS = 2 * IMAGES * PIXELS * CH * CH + 2 * IMAGES * PIXELS * CH * WORDS
 def tile_lvc_pa_t_kernel(tc, x, conv_w, conv_b, codebook, log_smooth, out_0, out_1):
     nc = tc.nc
     with ExitStack() as ctx:
+        ctx.enter_context(tc.manual_schedule())
         const = ctx.enter_context(tc.tile_pool(name="const", bufs=1))
         xin = ctx.enter_context(tc.tile_pool(name="xin", bufs=1))
         two = ctx.enter_context(tc.tile_pool(name="two", bufs=2))
         three = ctx.enter_context(tc.tile_pool(name="three", bufs=3))
         four = ctx.enter_context(tc.tile_pool(name="four", bufs=4))
-        psum_y = ctx.enter_context(tc.psum_pool(name="psum_y", bufs=3))
+        six = ctx.enter_context(tc.tile_pool(name="six", bufs=6))
+        psum_y = ctx.enter_context(tc.psum_pool(name="psum_y", bufs=4))
         psum_t = ctx.enter_context(tc.psum_pool(name="psum_t", bufs=3))
         psum_c = ctx.enter_context(tc.psum_pool(name="psum_c", bufs=1))
-        psum_s = ctx.enter_context(tc.psum_pool(name="psum_s", bufs=1))
 
         w_raw = const.tile([P, 4 * CH], BF16)
         nc.sync.dma_start(
@@ -46,9 +46,9 @@ def tile_lvc_pa_t_kernel(tc, x, conv_w, conv_b, codebook, log_smooth, out_0, out
         cb_raw = const.tile([P, CH], BF16)
         nc.scalar.dma_start(out=cb_raw[:], in_=codebook)
 
-        zrow = const.tile([P, CH + WORDS], BF16)
+        zrow = const.tile([P, 768], BF16)
         nc.vector.memset(zrow[:], 0.0)
-        ones = const.tile([P, 2 * P], BF16)
+        ones = const.tile([P, P], BF16)
         nc.vector.memset(ones[:], 1.0)
         warm_in = const.tile([P, 1], F32)
         nc.vector.memset(warm_in[:], 0.0)
@@ -75,11 +75,34 @@ def tile_lvc_pa_t_kernel(tc, x, conv_w, conv_b, codebook, log_smooth, out_0, out
         warm_out = const.tile([P, 1], F32)
         nc.scalar.activation(out=warm_out[:], in_=warm_in[:], func=ACT.Exp)
 
+        w_words = w_raw[:].bitcast(F32)
+        w_grouped = const.tile([P, 4 * CH], BF16, align_bytes=64)
+        w_grouped_words = w_grouped[:].bitcast(F32)
+        w_banks = []
+        for h in range(2):
+            w_t = psum_t.tile([P, 4, P], F32, tag="xt")
+            for a in range(2):
+                for u in range(2):
+                    col = (2 * h + a) * 256 + u * P
+                    nc.tensor.transpose(w_t[:, 2 * a + u, :], w_words[:, col : col + P], ident[:])
+            w_banks.append(w_t)
+        for h in range(2):
+            dst = w_grouped_words[:, 512 * h : 512 * (h + 1)].rearrange("p (a o u) -> p a o u", a=2, u=2)
+            src = w_banks[h][:].rearrange("p (a u) o -> p a o u", a=2)
+            if h == 0:
+                nc.vector.tensor_copy(out=dst, in_=src)
+            else:
+                nc.scalar.copy(out=dst, in_=src)
+
         cb_f32 = const.tile([P, CH], F32)
         nc.scalar.copy(out=cb_f32[:], in_=cb_raw[:])
         cb_t = psum_t.tile([P, 4, P], F32, tag="xt")
         for t in range(4):
             nc.tensor.transpose(cb_t[:, t, :], cb_f32[:, P * t : P * (t + 1)], ident[:])
+        bias_ps = psum_y.tile([P, CH], F32, tag="y")
+        nc.tensor.matmul(out=bias_ps[:], lhsT=ones[:], rhs=zrow[:, 0:CH], start=True, stop=True)
+        bias_bc = const.tile([P, CH], F32)
+        nc.scalar.copy(out=bias_bc[:], in_=bias_ps[:])
         cb_sq = const.tile([P, CH], BF16)
         c2col = const.tile([P, 1], F32)
         nc.scalar.activation(out=cb_sq[:], in_=cb_raw[:], func=ACT.Square, accum_out=c2col[:])
@@ -88,36 +111,47 @@ def tile_lvc_pa_t_kernel(tc, x, conv_w, conv_b, codebook, log_smooth, out_0, out
         cb_grouped = const.tile([P, WORDS, 4], BF16, align_bytes=64)
         nc.scalar.copy(out=cb_grouped[:], in_=cb_t[:].rearrange("p t k -> p k t"))
 
-        w_words = w_raw[:].bitcast(F32)
-        w_grouped = const.tile([P, 4 * CH], BF16, align_bytes=64)
-        w_grouped_words = w_grouped[:].bitcast(F32)
-        for h in range(2):
-            w_t = psum_t.tile([P, 4, P], F32, tag="xt")
-            for a in range(2):
-                for u in range(2):
-                    col = (2 * h + a) * 256 + u * P
-                    nc.tensor.transpose(w_t[:, 2 * a + u, :], w_words[:, col : col + P], ident[:])
-            dst = w_grouped_words[:, 512 * h : 512 * (h + 1)].rearrange("p (a o u) -> p a o u", a=2, u=2)
-            src = w_t[:].rearrange("p (a u) o -> p a o u", a=2)
-            if h == 0:
-                nc.vector.tensor_copy(out=dst, in_=src)
-            else:
-                nc.scalar.copy(out=dst, in_=src)
-
+        w_codes = const.tile([P, CH], U32, align_bytes=64)
+        w_scales = const.tile([P, CH], U8, align_bytes=64)
         cb_codes = const.tile([P, WORDS], U32, align_bytes=64)
         cb_scales = const.tile([P, WORDS], U8, align_bytes=64)
-        nc.vector.quantize_mx(
-            out=cb_codes[:].bitcast(FP8X4), scales=cb_scales[:], in_=cb_grouped[:].rearrange("p k t -> p (k t)")
-        )
+        s_bc = const.tile([P, WORDS], F32)
+        c2_bc = const.tile([P, TILES, WORDS], F32)
 
-        grouped = {}
-        codes = {}
-        scales = {}
+        def quantise_w():
+            nc.vector.quantize_mx(out=w_codes[:].bitcast(FP8X4), scales=w_scales[:], in_=w_grouped[:])
+
+        def quantise_cb():
+            nc.vector.quantize_mx(
+                out=cb_codes[:].bitcast(FP8X4), scales=cb_scales[:], in_=cb_grouped[:].rearrange("p k t -> p (k t)")
+            )
+
+        def spread_constants():
+            ls_ps = psum_t.tile([P, 4, P], F32, tag="xt")
+            nc.tensor.matmul(
+                out=ls_ps[:, 0:2, :].rearrange("p a k -> p (a k)"),
+                lhsT=ones[:],
+                rhs=zrow[:, CH:768],
+                start=True,
+                stop=True,
+            )
+            nc.scalar.activation(out=s_bc[:], in_=ls_ps[:, 0, :], func=ACT.Exp)
+            c2_ps = psum_c.tile([P, TILES, WORDS], F32, tag="xc")
+            nc.tensor.transpose(c2_ps[:, 0, :], c2rep[:], ident[:])
+            nc.scalar.copy(out=c2_bc[:], in_=c2_ps[:, 0:1, :].to_broadcast([P, TILES, WORDS]))
+
+        x_grouped = {}
+        x_codes = {}
+        x_scales = {}
         y_banks = {}
         xp = {}
         x2 = {}
         xt_banks = {}
+        xp_grouped = {}
+        xp_codes = {}
+        xp_scales = {}
         xc_banks = {}
+        part = {}
         dist = {}
         dmin = {}
         expo = {}
@@ -127,46 +161,37 @@ def tile_lvc_pa_t_kernel(tc, x, conv_w, conv_b, codebook, log_smooth, out_0, out
         def live(g):
             return 0 <= g < GROUPS
 
-        def grouped_tile(m):
-            if m not in grouped:
-                pair = three.tile([P, 2, GROUP * 4], BF16, align_bytes=64, tag="grouped")
-                grouped[m] = pair
-            return grouped[m]
-
         def regroup_x(g):
             if not live(g):
                 return
             n0 = GROUP * (g % 2)
-            half = grouped_tile(g)[:, 0, :].rearrange("p (n t) -> p n t", t=4)
+            grouped = two.tile([P, GROUP, 4], BF16, align_bytes=64, tag="x_grouped")
             if g < VECTOR_REGROUPS:
                 nc.vector.tensor_copy(
-                    out=half.rearrange("p (c i) t -> p c t i", i=4),
+                    out=grouped[:].rearrange("p (c i) t -> p c t i", i=4),
                     in_=raw[g // 2][:, :, n0 : n0 + GROUP].rearrange("p t (c i) -> p c t i", i=4),
                 )
             else:
                 nc.gpsimd.tensor_scalar(
-                    out=half,
+                    out=grouped[:],
                     in0=raw[g // 2][:, :, n0 : n0 + GROUP].rearrange("p t n -> p n t"),
                     scalar1=1.0,
                     scalar2=0.0,
                     op0=ALU.mult,
                     op1=ALU.add,
                 )
+            x_grouped[g] = grouped
 
-        def quantise(m):
-            lo = 0 if live(m) else 1
-            hi = 2 if live(m - LAG) else 1
-            if lo >= hi:
+        def quantise_x(g):
+            if not live(g):
                 return
-            c_tile = two.tile([P, 2, GROUP], U32, align_bytes=64, tag="codes")
-            s_tile = two.tile([P, 2, GROUP], U8, align_bytes=64, tag="scales")
+            codes = two.tile([P, GROUP], U32, align_bytes=64, tag="x_codes")
+            scales = two.tile([P, GROUP], U8, align_bytes=64, tag="x_scales")
             nc.vector.quantize_mx(
-                out=c_tile[:, lo:hi, :].rearrange("p a n -> p (a n)").bitcast(FP8X4),
-                scales=s_tile[:, lo:hi, :].rearrange("p a n -> p (a n)"),
-                in_=grouped[m][:, lo:hi, :].rearrange("p a n -> p (a n)"),
+                out=codes[:].bitcast(FP8X4), scales=scales[:], in_=x_grouped[g][:].rearrange("p n t -> p (n t)")
             )
-            codes[m] = c_tile
-            scales[m] = s_tile
+            x_codes[g] = codes
+            x_scales[g] = scales
 
         def conv(g):
             if not live(g):
@@ -175,8 +200,8 @@ def tile_lvc_pa_t_kernel(tc, x, conv_w, conv_b, codebook, log_smooth, out_0, out
                 y = psum_y.tile([P, CH], F32, tag="y")
                 nc.tensor.matmul_mx(
                     out=y[:],
-                    lhsT=codes[g][:, 0, P * j : P * (j + 1)].bitcast(FP8X4),
-                    lhsT_scale=scales[g][:, 0, P * j : P * (j + 1)],
+                    lhsT=x_codes[g][:, P * j : P * (j + 1)].bitcast(FP8X4),
+                    lhsT_scale=x_scales[g][:, P * j : P * (j + 1)],
                     rhs=w_codes[:].bitcast(FP8X4),
                     rhs_scale=w_scales[:],
                     start=True,
@@ -184,37 +209,51 @@ def tile_lvc_pa_t_kernel(tc, x, conv_w, conv_b, codebook, log_smooth, out_0, out
                 )
                 y_banks[(g, j)] = y
 
-        def add_bias(g, j):
-            if j == 0:
-                xp_tile = three.tile([P, TILES, CH], F32, tag="xp")
-                xp[g] = xp_tile
-                x2_tile = four.tile([P, TILES], F32, tag="x2")
-                x2[g] = x2_tile
-            nc.vector.tensor_tensor(out=xp[g][:, j, :], in0=y_banks[(g, j)][:], in1=bias_bc[:], op=ALU.add)
-
-        def transposes(g, j):
-            xt = psum_t.tile([P, 4, P], F32, tag="xt")
-            for t in range(4):
-                nc.tensor.transpose(xt[:, t, :], xp[g][:, j, P * t : P * (t + 1)], ident[:])
-            xt_banks[(g, j)] = xt
+        def add_bias_and_transpose(g):
+            if not live(g):
+                return
+            xp_tile = four.tile([P, TILES, CH], F32, tag="xp")
+            xp[g] = xp_tile
+            for j in range(TILES):
+                nc.vector.tensor_tensor(out=xp_tile[:, j, :], in0=y_banks[(g, j)][:], in1=bias_bc[:], op=ALU.add)
+                xt = psum_t.tile([P, 4, P], F32, tag="xt")
+                for t in range(4):
+                    nc.tensor.transpose(xt[:, t, :], xp_tile[:, j, P * t : P * (t + 1)], ident[:])
+                xt_banks[(g, j)] = xt
+            n0 = GROUP * (g % 2)
+            nc.sync.dma_start(
+                out=out_0[g // 2, n0 : n0 + GROUP, :].rearrange("(j p) o -> p j o", p=P), in_=xp_tile[:]
+            )
 
         def sum_squares(g, j):
+            if not live(g):
+                return
+            if j == 0:
+                x2_tile = six.tile([P, TILES], F32, tag="x2")
+                x2[g] = x2_tile
             junk = two.tile([P, CH], BF16, tag="junk")
             nc.scalar.activation(out=junk[:], in_=xp[g][:, j, :], func=ACT.Square, accum_out=x2[g][:, j : j + 1])
 
-        def regroup_xp(g, j):
-            dst = grouped_tile(g + LAG)[:, 1, 4 * P * j : 4 * P * (j + 1)].rearrange("p (n t) -> p n t", t=4)
-            src = xt_banks[(g, j)][:].rearrange("p t n -> p n t")
-            if j == TILES - 1 and g % 4 != 0:
-                nc.vector.tensor_copy(out=dst, in_=src)
-            else:
-                nc.scalar.copy(out=dst, in_=src)
+        def regroup_xp(g):
+            if not live(g):
+                return
+            grouped = three.tile([P, TILES, P, 4], BF16, align_bytes=64, tag="xp_grouped")
+            xp_grouped[g] = grouped
+            for j in range(TILES):
+                nc.scalar.copy(out=grouped[:, j, :, :], in_=xt_banks[(g, j)][:].rearrange("p t n -> p n t"))
 
-        def store_xp(g):
-            n0 = GROUP * (g % 2)
-            nc.sync.dma_start(
-                out=out_0[g // 2, n0 : n0 + GROUP, :].rearrange("(j p) o -> p j o", p=P), in_=xp[g][:]
+        def quantise_xp(g):
+            if not live(g):
+                return
+            codes = two.tile([P, GROUP], U32, align_bytes=64, tag="xp_codes")
+            scales = two.tile([P, GROUP], U8, align_bytes=64, tag="xp_scales")
+            nc.vector.quantize_mx(
+                out=codes[:].bitcast(FP8X4),
+                scales=scales[:],
+                in_=xp_grouped[g][:].rearrange("p j n t -> p (j n t)"),
             )
+            xp_codes[g] = codes
+            xp_scales[g] = scales
 
         def cross(g):
             if not live(g):
@@ -223,8 +262,8 @@ def tile_lvc_pa_t_kernel(tc, x, conv_w, conv_b, codebook, log_smooth, out_0, out
             for j in range(TILES):
                 nc.tensor.matmul_mx(
                     out=xc[:, j, :],
-                    lhsT=codes[g + LAG][:, 1, P * j : P * (j + 1)].bitcast(FP8X4),
-                    lhsT_scale=scales[g + LAG][:, 1, P * j : P * (j + 1)],
+                    lhsT=xp_codes[g][:, P * j : P * (j + 1)].bitcast(FP8X4),
+                    lhsT_scale=xp_scales[g][:, P * j : P * (j + 1)],
                     rhs=cb_codes[:].bitcast(FP8X4),
                     rhs_scale=cb_scales[:],
                     start=True,
@@ -232,37 +271,46 @@ def tile_lvc_pa_t_kernel(tc, x, conv_w, conv_b, codebook, log_smooth, out_0, out
                 )
             xc_banks[g] = xc
 
-        def distances(g):
+        def distance_first(g):
             if not live(g):
                 return
-            part = two.tile([P, TILES, WORDS], F32, tag="part")
+            u_tile = two.tile([P, TILES, WORDS], F32, tag="part")
             nc.vector.scalar_tensor_tensor(
-                out=part[:].rearrange("p j k -> p (j k)"),
+                out=u_tile[:].rearrange("p j k -> p (j k)"),
                 in0=xc_banks[g][:].rearrange("p j k -> p (j k)"),
                 scalar=-2.0,
                 in1=c2_bc[:].rearrange("p j k -> p (j k)"),
                 op0=ALU.mult,
                 op1=ALU.add,
             )
-            scaled = two.tile([P, TILES, WORDS], F32, tag="scaled")
+            part[g] = u_tile
+
+        def distance_second(g):
+            if not live(g):
+                return
+            scaled = three.tile([P, TILES, WORDS], F32, tag="scaled")
             for j in range(TILES):
                 nc.vector.scalar_tensor_tensor(
                     out=scaled[:, j, :],
-                    in0=part[:, j, :],
+                    in0=part[g][:, j, :],
                     scalar=x2[g][:, j : j + 1],
-                    in1=s_ps[:, 0:WORDS],
+                    in1=s_bc[:],
                     op0=ALU.add,
                     op1=ALU.mult,
                 )
-            least = three.tile([P, TILES], F32, tag="least")
-            nc.vector.tensor_reduce(out=least[:], in_=scaled[:], axis=mybir.AxisListType.X, op=ALU.min)
             dist[g] = scaled
+
+        def row_minimum(g):
+            if not live(g):
+                return
+            least = three.tile([P, TILES], F32, tag="least")
+            nc.vector.tensor_reduce(out=least[:], in_=dist[g][:], axis=mybir.AxisListType.X, op=ALU.min)
             dmin[g] = least
 
         def exponent(g):
             if not live(g):
                 return
-            e = two.tile([P, TILES, WORDS], F32, tag="expo")
+            e = three.tile([P, TILES, WORDS], F32, tag="expo")
             total = three.tile([P, TILES], F32, tag="esum")
             for j in range(TILES):
                 nc.scalar.activation(
@@ -288,14 +336,9 @@ def tile_lvc_pa_t_kernel(tc, x, conv_w, conv_b, codebook, log_smooth, out_0, out
                 return
             assign = three.tile([P, TILES, WORDS], F32, tag="assign")
             for j in range(TILES):
-                if False:
-                    nc.gpsimd.tensor_scalar(
-                        out=assign[:, j, :],
-                        in0=expo[g][:, j, :],
-                        scalar1=rsum[g][:, j : j + 1],
-                        scalar2=0.0,
-                        op0=ALU.mult,
-                        op1=ALU.add,
+                if g % 4 != 0:
+                    nc.vector.tensor_scalar_mul(
+                        out=assign[:, j, :], in0=expo[g][:, j, :], scalar1=rsum[g][:, j : j + 1]
                     )
                 else:
                     nc.scalar.activation(
@@ -306,50 +349,27 @@ def tile_lvc_pa_t_kernel(tc, x, conv_w, conv_b, codebook, log_smooth, out_0, out
                 out=out_1[g // 2, n0 : n0 + GROUP, :].rearrange("(j p) k -> p j k", p=P), in_=assign[:]
             )
 
-        regroup_x(0)
-        w_codes = const.tile([P, CH], U32, align_bytes=64)
-        w_scales = const.tile([P, CH], U8, align_bytes=64)
-        nc.vector.quantize_mx(out=w_codes[:].bitcast(FP8X4), scales=w_scales[:], in_=w_grouped[:])
-        regroup_x(1)
-        quantise(0)
-
-        bias_ps = psum_y.tile([P, CH], F32, tag="y")
-        nc.tensor.matmul(out=bias_ps[:], lhsT=ones[:, 0:P], rhs=zrow[:, 0:CH], start=True, stop=True)
-        bias_bc = const.tile([P, CH], F32)
-        nc.scalar.copy(out=bias_bc[:], in_=bias_ps[:])
-        ls_ps = psum_t.tile([P, 4, P], F32, tag="xt")
-        nc.tensor.matmul(
-            out=ls_ps[:, 0:2, :].rearrange("p a k -> p (a k)"),
-            lhsT=zrow[:, CH : CH + WORDS],
-            rhs=ones[:],
-            start=True,
-            stop=True,
-        )
-        s_rep = const.tile([P, P], F32)
-        nc.scalar.activation(out=s_rep[:], in_=ls_ps[:, 0, :], func=ACT.Exp)
-        s_ps = psum_s.tile([P, CH], F32, tag="s")
-        nc.tensor.transpose(s_ps[:, 0:WORDS], s_rep[:], ident[:])
-        c2_ps = psum_c.tile([P, TILES, WORDS], F32, tag="xc")
-        nc.tensor.transpose(c2_ps[:, 0, :], c2rep[:], ident[:])
-        c2_bc = const.tile([P, TILES, WORDS], F32)
-        nc.scalar.copy(out=c2_bc[:], in_=c2_ps[:, 0:1, :].to_broadcast([P, TILES, WORDS]))
-        conv(0)
-
-        for it in range(GROUPS + 5):
-            normalise(it - 4)
-            exponent(it - 3)
-            if live(it):
-                for j in range(TILES):
-                    add_bias(it, j)
-                    transposes(it, j)
-                    sum_squares(it, j)
-                    if j >= 1:
-                        regroup_xp(it, j - 1)
-                regroup_xp(it, TILES - 1)
-                store_xp(it)
-            quantise(it + 1)
-            conv(it + 1)
-            distances(it - 2)
-            cross(it - 1)
-            regroup_x(it + 2)
-            reciprocal(it - 3)
+        for i in range(-1, GROUPS + 6):
+            if i == 0:
+                spread_constants()
+            sum_squares(i - 2, 2)
+            regroup_x(i + 1)
+            if i == -1:
+                quantise_w()
+            if i == 1:
+                quantise_cb()
+            sum_squares(i - 1, 1)
+            reciprocal(i - 5)
+            add_bias_and_transpose(i)
+            exponent(i - 4)
+            sum_squares(i, 0)
+            distance_second(i - 3)
+            quantise_xp(i - 1)
+            cross(i - 1)
+            normalise(i - 5)
+            quantise_x(i + 1)
+            conv(i + 1)
+            row_minimum(i - 3)
+            distance_first(i - 1)
+            sum_squares(i - 2, 3)
+            regroup_xp(i)

@@ -234,13 +234,13 @@ def tile_lvc_pa_t_kernel(tc, x, conv_w, conv_b, codebook, log_smooth, out_0, out
             junk = two.tile([P, CH], BF16, tag="junk")
             nc.scalar.activation(out=junk[:], in_=xp[g][:, j, :], func=ACT.Square, accum_out=x2[g][:, j : j + 1])
 
-        def regroup_xp(g):
+        def regroup_xp(g, j):
             if not live(g):
                 return
-            grouped = three.tile([P, TILES, P, 4], BF16, align_bytes=64, tag="xp_grouped")
-            xp_grouped[g] = grouped
-            for j in range(TILES):
-                nc.scalar.copy(out=grouped[:, j, :, :], in_=xt_banks[(g, j)][:].rearrange("p t n -> p n t"))
+            if j == 0:
+                grouped = three.tile([P, TILES, P, 4], BF16, align_bytes=64, tag="xp_grouped")
+                xp_grouped[g] = grouped
+            nc.scalar.copy(out=xp_grouped[g][:, j, :, :], in_=xt_banks[(g, j)][:].rearrange("p t n -> p n t"))
 
         def quantise_xp(g):
             if not live(g):
@@ -352,17 +352,16 @@ def tile_lvc_pa_t_kernel(tc, x, conv_w, conv_b, codebook, log_smooth, out_0, out
         for i in range(-1, GROUPS + 6):
             if i == 0:
                 spread_constants()
-            sum_squares(i - 2, 2)
+            sum_squares(i - 1, 1)
+            sum_squares(i - 1, 2)
+            exponent(i - 4)
             regroup_x(i + 1)
             if i == -1:
                 quantise_w()
             if i == 1:
                 quantise_cb()
-            sum_squares(i - 1, 1)
             reciprocal(i - 5)
             add_bias_and_transpose(i)
-            exponent(i - 4)
-            sum_squares(i, 0)
             distance_second(i - 3)
             quantise_xp(i - 1)
             cross(i - 1)
@@ -371,5 +370,9 @@ def tile_lvc_pa_t_kernel(tc, x, conv_w, conv_b, codebook, log_smooth, out_0, out
             conv(i + 1)
             row_minimum(i - 3)
             distance_first(i - 1)
-            sum_squares(i - 2, 3)
-            regroup_xp(i)
+            regroup_xp(i, 0)
+            regroup_xp(i, 1)
+            sum_squares(i - 1, 3)
+            regroup_xp(i, 2)
+            sum_squares(i, 0)
+            regroup_xp(i, 3)

@@ -19,7 +19,7 @@ WORDS = 128
 GROUP = 512
 TILES = GROUP // P
 GROUPS = IMAGES * PIXELS // GROUP
-VECTOR_REGROUPS = 2
+VECTOR_REGROUPS = 1
 
 FLOPS = 2 * IMAGES * PIXELS * CH * CH + 2 * IMAGES * PIXELS * CH * WORDS
 
@@ -30,13 +30,13 @@ def tile_lvc_pa_t_kernel(tc, x, conv_w, conv_b, codebook, log_smooth, out_0, out
         ctx.enter_context(tc.manual_schedule())
         const = ctx.enter_context(tc.tile_pool(name="const", bufs=1))
         xin = ctx.enter_context(tc.tile_pool(name="xin", bufs=1))
+        one = ctx.enter_context(tc.tile_pool(name="one", bufs=1))
         two = ctx.enter_context(tc.tile_pool(name="two", bufs=2))
         three = ctx.enter_context(tc.tile_pool(name="three", bufs=3))
         four = ctx.enter_context(tc.tile_pool(name="four", bufs=4))
         six = ctx.enter_context(tc.tile_pool(name="six", bufs=6))
         psum_y = ctx.enter_context(tc.psum_pool(name="psum_y", bufs=4))
-        psum_t = ctx.enter_context(tc.psum_pool(name="psum_t", bufs=3))
-        psum_c = ctx.enter_context(tc.psum_pool(name="psum_c", bufs=1))
+        psum_t = ctx.enter_context(tc.psum_pool(name="psum_t", bufs=4))
 
         w_raw = const.tile([P, 4 * CH], BF16)
         nc.sync.dma_start(
@@ -136,7 +136,7 @@ def tile_lvc_pa_t_kernel(tc, x, conv_w, conv_b, codebook, log_smooth, out_0, out
                 stop=True,
             )
             nc.scalar.activation(out=s_bc[:], in_=ls_ps[:, 0, :], func=ACT.Exp)
-            c2_ps = psum_c.tile([P, TILES, WORDS], F32, tag="xc")
+            c2_ps = psum_t.tile([P, TILES, WORDS], F32, tag="xt")
             nc.tensor.transpose(c2_ps[:, 0, :], c2rep[:], ident[:])
             nc.scalar.copy(out=c2_bc[:], in_=c2_ps[:, 0:1, :].to_broadcast([P, TILES, WORDS]))
 
@@ -165,7 +165,7 @@ def tile_lvc_pa_t_kernel(tc, x, conv_w, conv_b, codebook, log_smooth, out_0, out
             if not live(g):
                 return
             n0 = GROUP * (g % 2)
-            grouped = two.tile([P, GROUP, 4], BF16, align_bytes=64, tag="x_grouped")
+            grouped = one.tile([P, GROUP, 4], BF16, align_bytes=64, tag="x_grouped")
             if g < VECTOR_REGROUPS:
                 nc.vector.tensor_copy(
                     out=grouped[:].rearrange("p (c i) t -> p c t i", i=4),
@@ -258,7 +258,7 @@ def tile_lvc_pa_t_kernel(tc, x, conv_w, conv_b, codebook, log_smooth, out_0, out
         def cross(g):
             if not live(g):
                 return
-            xc = psum_c.tile([P, TILES, WORDS], F32, tag="xc")
+            xc = psum_y.tile([P, TILES, WORDS], F32, tag="y")
             for j in range(TILES):
                 nc.tensor.matmul_mx(
                     out=xc[:, j, :],
@@ -362,17 +362,15 @@ def tile_lvc_pa_t_kernel(tc, x, conv_w, conv_b, codebook, log_smooth, out_0, out
                 quantise_cb()
             reciprocal(i - 5)
             add_bias_and_transpose(i)
-            distance_second(i - 3)
             quantise_xp(i - 1)
             cross(i - 1)
+            distance_second(i - 3)
             normalise(i - 5)
             quantise_x(i + 1)
             conv(i + 1)
             row_minimum(i - 3)
             distance_first(i - 1)
-            regroup_xp(i, 0)
-            regroup_xp(i, 1)
+            for j in range(TILES):
+                regroup_xp(i, j)
             sum_squares(i - 1, 3)
-            regroup_xp(i, 2)
             sum_squares(i, 0)
-            regroup_xp(i, 3)

@@ -365,9 +365,9 @@ def tile_lvc_pa_t_kernel(tc, x, conv_w, conv_b, codebook, log_smooth, out_0, out
             quantise_xp(i - 1)
             cross(i - 1)
             distance_second(i - 3)
-            normalise(i - 5)
             quantise_x(i + 1)
             conv(i + 1)
+            normalise(i - 5)
             row_minimum(i - 3)
             distance_first(i - 1)
             for j in range(TILES):

@@ -20,6 +20,7 @@ GROUP = 512
 TILES = GROUP // P
 GROUPS = IMAGES * PIXELS // GROUP
 VECTOR_REGROUPS = 1
+GPSIMD_TILES = 2
 
 FLOPS = 2 * IMAGES * PIXELS * CH * CH + 2 * IMAGES * PIXELS * CH * WORDS
 
@@ -157,6 +158,7 @@ def tile_lvc_pa_t_kernel(tc, x, conv_w, conv_b, codebook, log_smooth, out_0, out
         expo = {}
         esum = {}
         rsum = {}
+        assign = {}
 
         def live(g):
             return 0 <= g < GROUPS
@@ -331,22 +333,36 @@ def tile_lvc_pa_t_kernel(tc, x, conv_w, conv_b, codebook, log_smooth, out_0, out
             nc.vector.reciprocal(out=r[:], in_=esum[g][:])
             rsum[g] = r
 
-        def normalise(g):
+        def normalise_first(g):
             if not live(g):
                 return
-            assign = three.tile([P, TILES, WORDS], F32, tag="assign")
-            for j in range(TILES):
-                if g % 4 != 0:
-                    nc.vector.tensor_scalar_mul(
-                        out=assign[:, j, :], in0=expo[g][:, j, :], scalar1=rsum[g][:, j : j + 1]
-                    )
-                else:
+            out_tile = three.tile([P, TILES, WORDS], F32, tag="assign")
+            for j in range(GPSIMD_TILES if g < GROUPS - 1 else 0):
+                nc.gpsimd.tensor_scalar(
+                    out=out_tile[:, j, :],
+                    in0=expo[g][:, j, :],
+                    scalar1=rsum[g][:, j : j + 1],
+                    scalar2=0.0,
+                    op0=ALU.mult,
+                    op1=ALU.add,
+                )
+            assign[g] = out_tile
+
+        def normalise_last(g):
+            if not live(g):
+                return
+            for j in range(GPSIMD_TILES, TILES):
+                nc.vector.tensor_scalar_mul(
+                    out=assign[g][:, j, :], in0=expo[g][:, j, :], scalar1=rsum[g][:, j : j + 1]
+                )
+            if g == GROUPS - 1:
+                for j in range(GPSIMD_TILES):
                     nc.scalar.activation(
-                        out=assign[:, j, :], in_=expo[g][:, j, :], func=ACT.Copy, scale=rsum[g][:, j : j + 1]
+                        out=assign[g][:, j, :], in_=expo[g][:, j, :], func=ACT.Copy, scale=rsum[g][:, j : j + 1]
                     )
             n0 = GROUP * (g % 2)
             nc.sync.dma_start(
-                out=out_1[g // 2, n0 : n0 + GROUP, :].rearrange("(j p) k -> p j k", p=P), in_=assign[:]
+                out=out_1[g // 2, n0 : n0 + GROUP, :].rearrange("(j p) k -> p j k", p=P), in_=assign[g][:]
             )
 
         for i in range(-1, GROUPS + 6):
@@ -361,13 +377,14 @@ def tile_lvc_pa_t_kernel(tc, x, conv_w, conv_b, codebook, log_smooth, out_0, out
             if i == 1:
                 quantise_cb()
             reciprocal(i - 5)
+            normalise_first(i - 5)
             add_bias_and_transpose(i)
             quantise_xp(i - 1)
             cross(i - 1)
             distance_second(i - 3)
             quantise_x(i + 1)
             conv(i + 1)
-            normalise(i - 5)
+            normalise_last(i - 5)
             row_minimum(i - 3)
             distance_first(i - 1)
             for j in range(TILES):

@@ -175,8 +175,8 @@ def tile_lvc_pa_t_kernel(tc, x, conv_w, conv_b, codebook, log_smooth, out_0, out
                 )
             else:
                 nc.gpsimd.tensor_scalar(
-                    out=grouped[:],
-                    in0=raw[g // 2][:, :, n0 : n0 + GROUP].rearrange("p t n -> p n t"),
+                    out=grouped[:].rearrange("p (c i) t -> p c t i", i=4),
+                    in0=raw[g // 2][:, :, n0 : n0 + GROUP].rearrange("p t (c i) -> p c t i", i=4),
                     scalar1=1.0,
                     scalar2=0.0,
                     op0=ALU.mult,

from contextlib import ExitStack

import concourse.mybir as mybir
from concourse.masks import make_identity

F32 = mybir.dt.float32
BF16 = mybir.dt.bfloat16
U32 = mybir.dt.uint32
U8 = mybir.dt.uint8
FP8X4 = mybir.dt.float8_e4m3fn_x4
ACT = mybir.ActivationFunctionType
ALU = mybir.AluOpType

P = 128
IMAGES = 8
CH = 512
PIXELS = 1024
WORDS = 128
GROUP = 512
TILES = GROUP // P
GROUPS = IMAGES * PIXELS // GROUP
VECTOR_REGROUPS = 1
GPSIMD_TILES = 2

FLOPS = 2 * IMAGES * PIXELS * CH * CH + 2 * IMAGES * PIXELS * CH * WORDS


def tile_lvc_pa_t_kernel(tc, x, conv_w, conv_b, codebook, log_smooth, out_0, out_1):
    nc = tc.nc
    with ExitStack() as ctx:
        ctx.enter_context(tc.manual_schedule())
        const = ctx.enter_context(tc.tile_pool(name="const", bufs=1))
        xin = ctx.enter_context(tc.tile_pool(name="xin", bufs=1))
        one = ctx.enter_context(tc.tile_pool(name="one", bufs=1))
        two = ctx.enter_context(tc.tile_pool(name="two", bufs=2))
        three = ctx.enter_context(tc.tile_pool(name="three", bufs=3))
        four = ctx.enter_context(tc.tile_pool(name="four", bufs=4))
        six = ctx.enter_context(tc.tile_pool(name="six", bufs=6))
        psum_y = ctx.enter_context(tc.psum_pool(name="psum_y", bufs=4))
        psum_t = ctx.enter_context(tc.psum_pool(name="psum_t", bufs=4))

        w_raw = const.tile([P, 4 * CH], BF16)
        nc.sync.dma_start(
            out=w_raw[:].rearrange("p (a c) -> p a c", a=4),
            in_=conv_w.rearrange("(a p) c -> p a c", p=P),
        )
        cb_raw = const.tile([P, CH], BF16)
        nc.scalar.dma_start(out=cb_raw[:], in_=codebook)

        zrow = const.tile([P, 768], BF16)
        nc.vector.memset(zrow[:], 0.0)
        ones = const.tile([P, P], BF16)
        nc.vector.memset(ones[:], 1.0)
        warm_in = const.tile([P, 1], F32)
        nc.vector.memset(warm_in[:], 0.0)
        nc.scalar.dma_start(out=zrow[0:1, 0:CH], in_=conv_b.rearrange("(o c) -> o c", o=1))
        nc.scalar.dma_start(out=zrow[0:1, CH : CH + WORDS], in_=log_smooth.rearrange("(o c) -> o c", o=1))

        raw = [xin.tile([P, 4, PIXELS], BF16, name="raw%d" % b) for b in range(IMAGES)]
        x0 = x[0].rearrange("(u p e) h w -> u p e (h w)", u=2, p=P, e=2)
        for half in range(2):
            for u in range(2):
                nc.sync.dma_start(
                    out=raw[0][:, 2 * u : 2 * u + 2, GROUP * half : GROUP * (half + 1)],
                    in_=x0[u][:, :, GROUP * half : GROUP * (half + 1)],
                )
        for b in range(1, IMAGES):
            nc.sync.dma_start(
                out=raw[b][:].rearrange("p (u e) n -> p u (e n)", u=2),
                in_=x[b].rearrange("(u p e) h w -> p u (e h w)", u=2, p=P, e=2),
            )

        ident = const.tile([P, P], F32)
        make_identity(nc, ident[:])

        warm_out = const.tile([P, 1], F32)
        nc.scalar.activation(out=warm_out[:], in_=warm_in[:], func=ACT.Exp)

        w_words = w_raw[:].bitcast(F32)
        w_grouped = const.tile([P, 4 * CH], BF16, align_bytes=64)
        w_grouped_words = w_grouped[:].bitcast(F32)
        w_banks = []
        for h in range(2):
            w_t = psum_t.tile([P, 4, P], F32, tag="xt")
            for a in range(2):
                for u in range(2):
                    col = (2 * h + a) * 256 + u * P
                    nc.tensor.transpose(w_t[:, 2 * a + u, :], w_words[:, col : col + P], ident[:])
            w_banks.append(w_t)
        for h in range(2):
            dst = w_grouped_words[:, 512 * h : 512 * (h + 1)].rearrange("p (a o u) -> p a o u", a=2, u=2)
            src = w_banks[h][:].rearrange("p (a u) o -> p a o u", a=2)
            if h == 0:
                nc.vector.tensor_copy(out=dst, in_=src)
            else:
                nc.scalar.copy(out=dst, in_=src)

        cb_f32 = const.tile([P, CH], F32)
        nc.scalar.copy(out=cb_f32[:], in_=cb_raw[:])
        cb_t = psum_t.tile([P, 4, P], F32, tag="xt")
        for t in range(4):
            nc.tensor.transpose(cb_t[:, t, :], cb_f32[:, P * t : P * (t + 1)], ident[:])
        bias_ps = psum_y.tile([P, CH], F32, tag="y")
        nc.tensor.matmul(out=bias_ps[:], lhsT=ones[:], rhs=zrow[:, 0:CH], start=True, stop=True)
        bias_bc = const.tile([P, CH], F32)
        nc.scalar.copy(out=bias_bc[:], in_=bias_ps[:])
        cb_sq = const.tile([P, CH], BF16)
        c2col = const.tile([P, 1], F32)
        nc.scalar.activation(out=cb_sq[:], in_=cb_raw[:], func=ACT.Square, accum_out=c2col[:])
        c2rep = const.tile([P, P], F32)
        nc.scalar.copy(out=c2rep[:], in_=c2col[:, 0:1].to_broadcast([P, P]))
        cb_grouped = const.tile([P, WORDS, 4], BF16, align_bytes=64)
        nc.scalar.copy(out=cb_grouped[:], in_=cb_t[:].rearrange("p t k -> p k t"))

        w_codes = const.tile([P, CH], U32, align_bytes=64)
        w_scales = const.tile([P, CH], U8, align_bytes=64)
        cb_codes = const.tile([P, WORDS], U32, align_bytes=64)
        cb_scales = const.tile([P, WORDS], U8, align_bytes=64)
        s_bc = const.tile([P, WORDS], F32)
        c2_bc = const.tile([P, TILES, WORDS], F32)

        def quantise_w():
            nc.vector.quantize_mx(out=w_codes[:].bitcast(FP8X4), scales=w_scales[:], in_=w_grouped[:])

        def quantise_cb():
            nc.vector.quantize_mx(
                out=cb_codes[:].bitcast(FP8X4), scales=cb_scales[:], in_=cb_grouped[:].rearrange("p k t -> p (k t)")
            )

        def spread_constants():
            ls_ps = psum_t.tile([P, 4, P], F32, tag="xt")
            nc.tensor.matmul(
                out=ls_ps[:, 0:2, :].rearrange("p a k -> p (a k)"),
                lhsT=ones[:],
                rhs=zrow[:, CH:768],
                start=True,
                stop=True,
            )
            nc.scalar.activation(out=s_bc[:], in_=ls_ps[:, 0, :], func=ACT.Exp)
            c2_ps = psum_t.tile([P, TILES, WORDS], F32, tag="xt")
            nc.tensor.transpose(c2_ps[:, 0, :], c2rep[:], ident[:])
            nc.scalar.copy(out=c2_bc[:], in_=c2_ps[:, 0:1, :].to_broadcast([P, TILES, WORDS]))

        x_grouped = {}
        x_codes = {}
        x_scales = {}
        y_banks = {}
        xp = {}
        x2 = {}
        xt_banks = {}
        xp_grouped = {}
        xp_codes = {}
        xp_scales = {}
        xc_banks = {}
        part = {}
        dist = {}
        dmin = {}
        expo = {}
        esum = {}
        rsum = {}
        assign = {}

        def live(g):
            return 0 <= g < GROUPS

        def regroup_x(g):
            if not live(g):
                return
            n0 = GROUP * (g % 2)
            grouped = one.tile([P, GROUP, 4], BF16, align_bytes=64, tag="x_grouped")
            if g < VECTOR_REGROUPS:
                nc.vector.tensor_copy(
                    out=grouped[:].rearrange("p (c i) t -> p c t i", i=4),
                    in_=raw[g // 2][:, :, n0 : n0 + GROUP].rearrange("p t (c i) -> p c t i", i=4),
                )
            else:
                nc.gpsimd.tensor_scalar(
                    out=grouped[:].rearrange("p (c i) t -> p c t i", i=4),
                    in0=raw[g // 2][:, :, n0 : n0 + GROUP].rearrange("p t (c i) -> p c t i", i=4),
                    scalar1=1.0,
                    scalar2=0.0,
                    op0=ALU.mult,
                    op1=ALU.add,
                )
            x_grouped[g] = grouped

        def quantise_x(g):
            if not live(g):
                return
            codes = two.tile([P, GROUP], U32, align_bytes=64, tag="x_codes")
            scales = two.tile([P, GROUP], U8, align_bytes=64, tag="x_scales")
            nc.vector.quantize_mx(
                out=codes[:].bitcast(FP8X4), scales=scales[:], in_=x_grouped[g][:].rearrange("p n t -> p (n t)")
            )
            x_codes[g] = codes
            x_scales[g] = scales

        def conv(g):
            if not live(g):
                return
            for j in range(TILES):
                y = psum_y.tile([P, CH], F32, tag="y")
                nc.tensor.matmul_mx(
                    out=y[:],
                    lhsT=x_codes[g][:, P * j : P * (j + 1)].bitcast(FP8X4),
                    lhsT_scale=x_scales[g][:, P * j : P * (j + 1)],
                    rhs=w_codes[:].bitcast(FP8X4),
                    rhs_scale=w_scales[:],
                    start=True,
                    stop=True,
                )
                y_banks[(g, j)] = y

        def add_bias_and_transpose(g):
            if not live(g):
                return
            xp_tile = four.tile([P, TILES, CH], F32, tag="xp")
            xp[g] = xp_tile
            for j in range(TILES):
                nc.vector.tensor_tensor(out=xp_tile[:, j, :], in0=y_banks[(g, j)][:], in1=bias_bc[:], op=ALU.add)
                xt = psum_t.tile([P, 4, P], F32, tag="xt")
                for t in range(4):
                    nc.tensor.transpose(xt[:, t, :], xp_tile[:, j, P * t : P * (t + 1)], ident[:])
                xt_banks[(g, j)] = xt
            n0 = GROUP * (g % 2)
            nc.sync.dma_start(
                out=out_0[g // 2, n0 : n0 + GROUP, :].rearrange("(j p) o -> p j o", p=P), in_=xp_tile[:]
            )

        def sum_squares(g, j):
            if not live(g):
                return
            if j == 0:
                x2_tile = six.tile([P, TILES], F32, tag="x2")
                x2[g] = x2_tile
            junk = two.tile([P, CH], BF16, tag="junk")
            nc.scalar.activation(out=junk[:], in_=xp[g][:, j, :], func=ACT.Square, accum_out=x2[g][:, j : j + 1])

        def regroup_xp(g, j):
            if not live(g):
                return
            if j == 0:
                grouped = three.tile([P, TILES, P, 4], BF16, align_bytes=64, tag="xp_grouped")
                xp_grouped[g] = grouped
            nc.scalar.copy(out=xp_grouped[g][:, j, :, :], in_=xt_banks[(g, j)][:].rearrange("p t n -> p n t"))

        def quantise_xp(g):
            if not live(g):
                return
            codes = two.tile([P, GROUP], U32, align_bytes=64, tag="xp_codes")
            scales = two.tile([P, GROUP], U8, align_bytes=64, tag="xp_scales")
            nc.vector.quantize_mx(
                out=codes[:].bitcast(FP8X4),
                scales=scales[:],
                in_=xp_grouped[g][:].rearrange("p j n t -> p (j n t)"),
            )
            xp_codes[g] = codes
            xp_scales[g] = scales

        def cross(g):
            if not live(g):
                return
            xc = psum_y.tile([P, TILES, WORDS], F32, tag="y")
            for j in range(TILES):
                nc.tensor.matmul_mx(
                    out=xc[:, j, :],
                    lhsT=xp_codes[g][:, P * j : P * (j + 1)].bitcast(FP8X4),
                    lhsT_scale=xp_scales[g][:, P * j : P * (j + 1)],
                    rhs=cb_codes[:].bitcast(FP8X4),
                    rhs_scale=cb_scales[:],
                    start=True,
                    stop=True,
                )
            xc_banks[g] = xc

        def distance_first(g):
            if not live(g):
                return
            u_tile = two.tile([P, TILES, WORDS], F32, tag="part")
            nc.vector.scalar_tensor_tensor(
                out=u_tile[:].rearrange("p j k -> p (j k)"),
                in0=xc_banks[g][:].rearrange("p j k -> p (j k)"),
                scalar=-2.0,
                in1=c2_bc[:].rearrange("p j k -> p (j k)"),
                op0=ALU.mult,
                op1=ALU.add,
            )
            part[g] = u_tile

        def distance_second(g):
            if not live(g):
                return
            scaled = three.tile([P, TILES, WORDS], F32, tag="scaled")
            for j in range(TILES):
                nc.vector.scalar_tensor_tensor(
                    out=scaled[:, j, :],
                    in0=part[g][:, j, :],
                    scalar=x2[g][:, j : j + 1],
                    in1=s_bc[:],
                    op0=ALU.add,
                    op1=ALU.mult,
                )
            dist[g] = scaled

        def row_minimum(g):
            if not live(g):
                return
            least = three.tile([P, TILES], F32, tag="least")
            nc.vector.tensor_reduce(out=least[:], in_=dist[g][:], axis=mybir.AxisListType.X, op=ALU.min)
            dmin[g] = least

        def exponent(g):
            if not live(g):
                return
            e = three.tile([P, TILES, WORDS], F32, tag="expo")
            total = three.tile([P, TILES], F32, tag="esum")
            for j in range(TILES):
                nc.scalar.activation(
                    out=e[:, j, :],
                    in_=dist[g][:, j, :],
                    func=ACT.Exp,
                    bias=dmin[g][:, j : j + 1],
                    scale=-1.0,
                    accum_out=total[:, j : j + 1],
                )
            expo[g] = e
            esum[g] = total

        def reciprocal(g):
            if not live(g):
                return
            r = three.tile([P, TILES], F32, tag="rsum")
            nc.vector.reciprocal(out=r[:], in_=esum[g][:])
            rsum[g] = r

        def normalise_first(g):
            if not live(g):
                return
            out_tile = three.tile([P, TILES, WORDS], F32, tag="assign")
            for j in range(GPSIMD_TILES if g < GROUPS - 1 else 0):
                nc.gpsimd.tensor_scalar(
                    out=out_tile[:, j, :],
                    in0=expo[g][:, j, :],
                    scalar1=rsum[g][:, j : j + 1],
                    scalar2=0.0,
                    op0=ALU.mult,
                    op1=ALU.add,
                )
            assign[g] = out_tile

        def normalise_last(g):
            if not live(g):
                return
            for j in range(GPSIMD_TILES, TILES):
                nc.vector.tensor_scalar_mul(
                    out=assign[g][:, j, :], in0=expo[g][:, j, :], scalar1=rsum[g][:, j : j + 1]
                )
            if g == GROUPS - 1:
                for j in range(GPSIMD_TILES):
                    nc.scalar.activation(
                        out=assign[g][:, j, :], in_=expo[g][:, j, :], func=ACT.Copy, scale=rsum[g][:, j : j + 1]
                    )
            n0 = GROUP * (g % 2)
            nc.sync.dma_start(
                out=out_1[g // 2, n0 : n0 + GROUP, :].rearrange("(j p) k -> p j k", p=P), in_=assign[g][:]
            )

        for i in range(-1, GROUPS + 6):
            if i == 0:
                spread_constants()
            sum_squares(i - 1, 1)
            sum_squares(i - 1, 2)
            exponent(i - 4)
            regroup_x(i + 1)
            if i == -1:
                quantise_w()
            if i == 1:
                quantise_cb()
            reciprocal(i - 5)
            normalise_first(i - 5)
            add_bias_and_transpose(i)
            quantise_xp(i - 1)
            cross(i - 1)
            distance_second(i - 3)
            quantise_x(i + 1)
            conv(i + 1)
            normalise_last(i - 5)
            row_minimum(i - 3)
            distance_first(i - 1)
            for j in range(TILES):
                regroup_xp(i, j)
            sum_squares(i - 1, 3)
            sum_squares(i, 0)
